import numpy as np
import ml_dtypes

BF16 = ml_dtypes.bfloat16


def bf(x):
    return np.asarray(x, np.float32).astype(BF16)


def f32(x):
    return np.asarray(x, np.float32)


def f64(x):
    return np.asarray(x).astype(np.float64)


def striped(idx):
    return np.tile(idx.reshape(-1, 16).T, (8, 1))


D, D2, S, R, N = 128, 256, 1024, 128, 256


def sigmoid(v):
    return 1.0 / (1.0 + np.exp(-v))


def setup_inputs():
    return {
        "table": bf(np.random.standard_normal((D, S))),
        "w_in": bf(np.random.standard_normal((D, D)) / np.sqrt(D)),
        "dyn": f32(0.5 * np.random.standard_normal((D, R))),
        "b_in": f32(0.2 * np.random.standard_normal((D, 1))),
        "h": bf(np.random.standard_normal((D, R))),
        "wf": bf(np.random.standard_normal((D2, D)) / np.sqrt(D2)),
        "b_f": f32(0.2 * np.random.standard_normal((D, 1))),
        "wh": bf(np.random.standard_normal((D2, D)) / np.sqrt(D2)),
        "b_h": f32(0.2 * np.random.standard_normal((D, 1))),
        "offs": striped(np.random.permutation(np.tile(np.arange(S), 2))[:N]),
    }


def reference(table, w_in, dyn, b_in, h, wf, b_f, wh, b_h, offs):
    idx = offs[:16].T.reshape(-1)
    proj = f64(w_in).T @ f64(table)[:, idx]
    x = 0.5 * (proj[:, :R] + proj[:, R:]) + f64(dyn) + f64(b_in)
    hh = f64(h)
    fg = sigmoid(f64(wf).T @ np.concatenate([hh, x], axis=0) + f64(b_f))
    ht = np.tanh(f64(wh).T @ np.concatenate([fg * hh, x], axis=0) + f64(b_h))
    return (1.0 - fg) * hh + fg * ht

@@ -1,0 +1,72 @@
+import concourse.mybir as mybir
+
+D = 128
+S = 1024
+R = 128
+N = 2 * R
+PER_COLUMN = 16
+
+BF16, F32, U16 = mybir.dt.bfloat16, mybir.dt.float32, mybir.dt.uint16
+ALU = mybir.AluOpType
+FUNC = mybir.ActivationFunctionType
+
+FLOPS = 2 * D * D * N + 2 * (2 * (2 * D) * D * R)
+
+
+def tile_tspddecoder_kernel(tc, table, w_in, dyn, b_in, h, wf, b_f, wh, b_h, offs, out):
+    nc = tc.nc
+    with (
+        tc.tile_pool(name="held", bufs=1) as held,
+        tc.psum_pool(name="psum", bufs=1) as psum,
+    ):
+        offsets = held.tile([D, N // PER_COLUMN], U16, name="offsets")
+        nc.sync.dma_start(offsets[:], offs)
+        table_sb = held.tile([D, S], BF16, name="table_sb")
+        nc.sync.dma_start(table_sb[:], table)
+        w_in_sb = held.tile([D, D], BF16, name="w_in_sb")
+        nc.scalar.dma_start(w_in_sb[:], w_in)
+        dyn_sb = held.tile([D, R], F32, name="dyn_sb")
+        nc.gpsimd.dma_start(dyn_sb[:], dyn)
+        b_in_sb = held.tile([D, 1], F32, name="b_in_sb")
+        nc.gpsimd.dma_start(b_in_sb[:], b_in)
+        h_sb = held.tile([D, R], BF16, name="h_sb")
+        nc.scalar.dma_start(h_sb[:], h)
+        wf_sb = held.tile([D, 2, D], BF16, name="wf_sb")
+        nc.scalar.dma_start(wf_sb[:], wf.rearrange("(b k) m -> k b m", b=2))
+        b_f_sb = held.tile([D, 1], F32, name="b_f_sb")
+        nc.gpsimd.dma_start(b_f_sb[:], b_f)
+        wh_sb = held.tile([D, 2, D], BF16, name="wh_sb")
+        nc.sync.dma_start(wh_sb[:], wh.rearrange("(b k) m -> k b m", b=2))
+        b_h_sb = held.tile([D, 1], F32, name="b_h_sb")
+        nc.gpsimd.dma_start(b_h_sb[:], b_h)
+
+        half = R // PER_COLUMN
+        proj = psum.tile([D, R], F32, name="proj")
+        nc.tensor.matmul(proj[:], w_in_sb[:], table_sb[:].indirect(offsets[:, 0:half]), start=True, stop=False)
+        nc.tensor.matmul(proj[:], w_in_sb[:], table_sb[:].indirect(offsets[:, half : 2 * half]), start=False, stop=True)
+        context = held.tile([D, R], F32, name="context")
+        nc.vector.tensor_scalar_add(context[:], dyn_sb[:], b_in_sb[:, 0:1])
+        x = held.tile([D, R], BF16, name="x")
+        nc.vector.scalar_tensor_tensor(x[:], proj[:], 0.5, context[:], ALU.mult, ALU.add)
+
+        f_sum = psum.tile([D, R], F32, name="f_sum")
+        nc.tensor.matmul(f_sum[:], wf_sb[:, 0, :], h_sb[:], start=True, stop=False)
+        nc.tensor.matmul(f_sum[:], wf_sb[:, 1, :], x[:], start=False, stop=True)
+        f = held.tile([D, R], F32, name="f")
+        nc.scalar.activation(f[:], f_sum[:], FUNC.Sigmoid, bias=b_f_sb[:, 0:1])
+
+        fh = held.tile([D, R], BF16, name="fh")
+        nc.vector.tensor_mul(fh[:], f[:], h_sb[:])
+        t_sum = psum.tile([D, R], F32, name="t_sum")
+        nc.tensor.matmul(t_sum[:], wh_sb[:, 1, :], x[:], start=True, stop=False)
+        nc.tensor.matmul(t_sum[:], wh_sb[:, 0, :], fh[:], start=False, stop=True)
+        t = held.tile([D, R], F32, name="t")
+        nc.scalar.activation(t[:], t_sum[:], FUNC.Tanh, bias=b_h_sb[:, 0:1])
+
+        minus_kept = held.tile([D, R], F32, name="minus_kept")
+        nc.vector.scalar_tensor_tensor(minus_kept[:], f[:], 1.0, h_sb[:], ALU.subtract, ALU.mult)
+        ft = held.tile([D, R], F32, name="ft")
+        nc.vector.tensor_mul(ft[:], f[:], t[:])
+        new_h = held.tile([D, R], F32, name="new_h")
+        nc.vector.tensor_sub(new_h[:], ft[:], minus_kept[:])
+        nc.sync.dma_start(out, new_h[:])

@@ -25,20 +25,25 @@ def tile_tspddecoder_kernel(tc, table, w_in, dyn, b_in, h, wf, b_f, wh, b_h, off
         nc.sync.dma_start(table_sb[:], table)
         w_in_sb = held.tile([D, D], BF16, name="w_in_sb")
         nc.scalar.dma_start(w_in_sb[:], w_in)
-        dyn_sb = held.tile([D, R], F32, name="dyn_sb")
-        nc.gpsimd.dma_start(dyn_sb[:], dyn)
         b_in_sb = held.tile([D, 1], F32, name="b_in_sb")
-        nc.gpsimd.dma_start(b_in_sb[:], b_in)
+        nc.scalar.dma_start(b_in_sb[:], b_in)
+        dyn_sb = held.tile([D, R], F32, name="dyn_sb")
+        nc.scalar.dma_start(dyn_sb[:], dyn)
         h_sb = held.tile([D, R], BF16, name="h_sb")
         nc.scalar.dma_start(h_sb[:], h)
         wf_sb = held.tile([D, 2, D], BF16, name="wf_sb")
         nc.scalar.dma_start(wf_sb[:], wf.rearrange("(b k) m -> k b m", b=2))
         b_f_sb = held.tile([D, 1], F32, name="b_f_sb")
-        nc.gpsimd.dma_start(b_f_sb[:], b_f)
+        nc.sync.dma_start(b_f_sb[:], b_f)
         wh_sb = held.tile([D, 2, D], BF16, name="wh_sb")
         nc.sync.dma_start(wh_sb[:], wh.rearrange("(b k) m -> k b m", b=2))
         b_h_sb = held.tile([D, 1], F32, name="b_h_sb")
-        nc.gpsimd.dma_start(b_h_sb[:], b_h)
+        nc.sync.dma_start(b_h_sb[:], b_h)
+
+        zeros = held.tile([D, 1], F32, name="zeros")
+        nc.vector.memset(zeros[:], 0.0)
+        warmed = held.tile([D, 1], F32, name="warmed")
+        nc.scalar.activation(warmed[:], zeros[:], FUNC.Sigmoid)
 
         half = R // PER_COLUMN
         proj = psum.tile([D, R], F32, name="proj")

@@ -40,11 +40,6 @@ def tile_tspddecoder_kernel(tc, table, w_in, dyn, b_in, h, wf, b_f, wh, b_h, off
         b_h_sb = held.tile([D, 1], F32, name="b_h_sb")
         nc.sync.dma_start(b_h_sb[:], b_h)
 
-        zeros = held.tile([D, 1], F32, name="zeros")
-        nc.vector.memset(zeros[:], 0.0)
-        warmed = held.tile([D, 1], F32, name="warmed")
-        nc.scalar.activation(warmed[:], zeros[:], FUNC.Sigmoid)
-
         half = R // PER_COLUMN
         proj = psum.tile([D, R], F32, name="proj")
         nc.tensor.matmul(proj[:], w_in_sb[:], table_sb[:].indirect(offsets[:, 0:half]), start=True, stop=False)

@@ -19,26 +19,31 @@ def tile_tspddecoder_kernel(tc, table, w_in, dyn, b_in, h, wf, b_f, wh, b_h, off
         tc.tile_pool(name="held", bufs=1) as held,
         tc.psum_pool(name="psum", bufs=1) as psum,
     ):
+        table_sb = held.tile([D, S], BF16, name="table_sb")
+        nc.scalar.dma_start(table_sb[:], table)
         offsets = held.tile([D, N // PER_COLUMN], U16, name="offsets")
         nc.sync.dma_start(offsets[:], offs)
-        table_sb = held.tile([D, S], BF16, name="table_sb")
-        nc.sync.dma_start(table_sb[:], table)
         w_in_sb = held.tile([D, D], BF16, name="w_in_sb")
-        nc.scalar.dma_start(w_in_sb[:], w_in)
-        b_in_sb = held.tile([D, 1], F32, name="b_in_sb")
-        nc.scalar.dma_start(b_in_sb[:], b_in)
-        dyn_sb = held.tile([D, R], F32, name="dyn_sb")
-        nc.scalar.dma_start(dyn_sb[:], dyn)
-        h_sb = held.tile([D, R], BF16, name="h_sb")
-        nc.scalar.dma_start(h_sb[:], h)
+        nc.sync.dma_start(w_in_sb[:], w_in)
+        wh_sb = held.tile([D, 2, D], BF16, name="wh_sb")
+        nc.gpsimd.dma_start(wh_sb[:], wh.rearrange("(b k) m -> k b m", b=2))
         wf_sb = held.tile([D, 2, D], BF16, name="wf_sb")
         nc.scalar.dma_start(wf_sb[:], wf.rearrange("(b k) m -> k b m", b=2))
+        b_in_sb = held.tile([D, 1], F32, name="b_in_sb")
+        nc.sync.dma_start(b_in_sb[:], b_in)
+        h_sb = held.tile([D, R], BF16, name="h_sb")
+        nc.scalar.dma_start(h_sb[:], h)
+        dyn_sb = held.tile([D, R], F32, name="dyn_sb")
+        nc.sync.dma_start(dyn_sb[:], dyn)
         b_f_sb = held.tile([D, 1], F32, name="b_f_sb")
         nc.sync.dma_start(b_f_sb[:], b_f)
-        wh_sb = held.tile([D, 2, D], BF16, name="wh_sb")
-        nc.sync.dma_start(wh_sb[:], wh.rearrange("(b k) m -> k b m", b=2))
         b_h_sb = held.tile([D, 1], F32, name="b_h_sb")
         nc.sync.dma_start(b_h_sb[:], b_h)
+
+        zeros = held.tile([D, 1], F32, name="zeros")
+        nc.vector.memset(zeros[:], 0.0)
+        warmed = held.tile([D, 1], F32, name="warmed")
+        nc.scalar.activation(warmed[:], zeros[:], FUNC.Sigmoid)
 
         half = R // PER_COLUMN
         proj = psum.tile([D, R], F32, name="proj")

@@ -5,6 +5,8 @@ S = 1024
 R = 128
 N = 2 * R
 PER_COLUMN = 16
+GROUPS = 2
+G = R // GROUPS
 
 BF16, F32, U16 = mybir.dt.bfloat16, mybir.dt.float32, mybir.dt.uint16
 ALU = mybir.AluOpType
@@ -19,31 +21,26 @@ def tile_tspddecoder_kernel(tc, table, w_in, dyn, b_in, h, wf, b_f, wh, b_h, off
         tc.tile_pool(name="held", bufs=1) as held,
         tc.psum_pool(name="psum", bufs=1) as psum,
     ):
-        table_sb = held.tile([D, S], BF16, name="table_sb")
-        nc.scalar.dma_start(table_sb[:], table)
         offsets = held.tile([D, N // PER_COLUMN], U16, name="offsets")
         nc.sync.dma_start(offsets[:], offs)
+        table_sb = held.tile([D, S], BF16, name="table_sb")
+        nc.sync.dma_start(table_sb[:], table)
         w_in_sb = held.tile([D, D], BF16, name="w_in_sb")
-        nc.sync.dma_start(w_in_sb[:], w_in)
-        wh_sb = held.tile([D, 2, D], BF16, name="wh_sb")
-        nc.gpsimd.dma_start(wh_sb[:], wh.rearrange("(b k) m -> k b m", b=2))
-        wf_sb = held.tile([D, 2, D], BF16, name="wf_sb")
-        nc.scalar.dma_start(wf_sb[:], wf.rearrange("(b k) m -> k b m", b=2))
+        nc.scalar.dma_start(w_in_sb[:], w_in)
         b_in_sb = held.tile([D, 1], F32, name="b_in_sb")
-        nc.sync.dma_start(b_in_sb[:], b_in)
+        nc.scalar.dma_start(b_in_sb[:], b_in)
+        dyn_sb = held.tile([D, R], F32, name="dyn_sb")
+        nc.scalar.dma_start(dyn_sb[:], dyn)
         h_sb = held.tile([D, R], BF16, name="h_sb")
         nc.scalar.dma_start(h_sb[:], h)
-        dyn_sb = held.tile([D, R], F32, name="dyn_sb")
-        nc.sync.dma_start(dyn_sb[:], dyn)
+        wf_sb = held.tile([D, 2, D], BF16, name="wf_sb")
+        nc.scalar.dma_start(wf_sb[:], wf.rearrange("(b k) m -> k b m", b=2))
         b_f_sb = held.tile([D, 1], F32, name="b_f_sb")
         nc.sync.dma_start(b_f_sb[:], b_f)
+        wh_sb = held.tile([D, 2, D], BF16, name="wh_sb")
+        nc.sync.dma_start(wh_sb[:], wh.rearrange("(b k) m -> k b m", b=2))
         b_h_sb = held.tile([D, 1], F32, name="b_h_sb")
         nc.sync.dma_start(b_h_sb[:], b_h)
-
-        zeros = held.tile([D, 1], F32, name="zeros")
-        nc.vector.memset(zeros[:], 0.0)
-        warmed = held.tile([D, 1], F32, name="warmed")
-        nc.scalar.activation(warmed[:], zeros[:], FUNC.Sigmoid)
 
         half = R // PER_COLUMN
         proj = psum.tile([D, R], F32, name="proj")
@@ -51,27 +48,40 @@ def tile_tspddecoder_kernel(tc, table, w_in, dyn, b_in, h, wf, b_f, wh, b_h, off
         nc.tensor.matmul(proj[:], w_in_sb[:], table_sb[:].indirect(offsets[:, half : 2 * half]), start=False, stop=True)
         context = held.tile([D, R], F32, name="context")
         nc.vector.tensor_scalar_add(context[:], dyn_sb[:], b_in_sb[:, 0:1])
+
+        groups = [slice(g * G, (g + 1) * G) for g in range(GROUPS)]
+        f_sum = [psum.tile([D, G], F32, name=f"f_sum{g}") for g in range(GROUPS)]
+        t_sum = [psum.tile([D, G], F32, name=f"t_sum{g}") for g in range(GROUPS)]
         x = held.tile([D, R], BF16, name="x")
-        nc.vector.scalar_tensor_tensor(x[:], proj[:], 0.5, context[:], ALU.mult, ALU.add)
-
-        f_sum = psum.tile([D, R], F32, name="f_sum")
-        nc.tensor.matmul(f_sum[:], wf_sb[:, 0, :], h_sb[:], start=True, stop=False)
-        nc.tensor.matmul(f_sum[:], wf_sb[:, 1, :], x[:], start=False, stop=True)
         f = held.tile([D, R], F32, name="f")
-        nc.scalar.activation(f[:], f_sum[:], FUNC.Sigmoid, bias=b_f_sb[:, 0:1])
-
         fh = held.tile([D, R], BF16, name="fh")
-        nc.vector.tensor_mul(fh[:], f[:], h_sb[:])
-        t_sum = psum.tile([D, R], F32, name="t_sum")
-        nc.tensor.matmul(t_sum[:], wh_sb[:, 1, :], x[:], start=True, stop=False)
-        nc.tensor.matmul(t_sum[:], wh_sb[:, 0, :], fh[:], start=False, stop=True)
         t = held.tile([D, R], F32, name="t")
-        nc.scalar.activation(t[:], t_sum[:], FUNC.Tanh, bias=b_h_sb[:, 0:1])
-
         minus_kept = held.tile([D, R], F32, name="minus_kept")
-        nc.vector.scalar_tensor_tensor(minus_kept[:], f[:], 1.0, h_sb[:], ALU.subtract, ALU.mult)
         ft = held.tile([D, R], F32, name="ft")
-        nc.vector.tensor_mul(ft[:], f[:], t[:])
         new_h = held.tile([D, R], F32, name="new_h")
-        nc.vector.tensor_sub(new_h[:], ft[:], minus_kept[:])
+
+        for cols in groups:
+            nc.vector.scalar_tensor_tensor(x[:, cols], proj[:, cols], 0.5, context[:, cols], ALU.mult, ALU.add)
+
+        for g, cols in enumerate(groups):
+            nc.tensor.matmul(f_sum[g][:], wf_sb[:, 0, :], h_sb[:, cols], start=True, stop=False)
+        for g, cols in enumerate(groups):
+            nc.tensor.matmul(f_sum[g][:], wf_sb[:, 1, :], x[:, cols], start=False, stop=True)
+        for g, cols in enumerate(groups):
+            nc.scalar.activation(f[:, cols], f_sum[g][:], FUNC.Sigmoid, bias=b_f_sb[:, 0:1])
+
+        for cols in groups:
+            nc.vector.tensor_mul(fh[:, cols], f[:, cols], h_sb[:, cols])
+        for g, cols in enumerate(groups):
+            nc.tensor.matmul(t_sum[g][:], wh_sb[:, 1, :], x[:, cols], start=True, stop=False)
+        for g, cols in enumerate(groups):
+            nc.tensor.matmul(t_sum[g][:], wh_sb[:, 0, :], fh[:, cols], start=False, stop=True)
+        for g, cols in enumerate(groups):
+            nc.scalar.activation(t[:, cols], t_sum[g][:], FUNC.Tanh, bias=b_h_sb[:, 0:1])
+
+        nc.vector.scalar_tensor_tensor(minus_kept[:], f[:], 1.0, h_sb[:], ALU.subtract, ALU.mult)
+        for cols in groups:
+            nc.vector.tensor_mul(ft[:, cols], f[:, cols], t[:, cols])
+        for cols in groups:
+            nc.vector.tensor_sub(new_h[:, cols], ft[:, cols], minus_kept[:, cols])
         nc.sync.dma_start(out, new_h[:])

@@ -23,18 +23,18 @@ def tile_tspddecoder_kernel(tc, table, w_in, dyn, b_in, h, wf, b_f, wh, b_h, off
     ):
         offsets = held.tile([D, N // PER_COLUMN], U16, name="offsets")
         nc.sync.dma_start(offsets[:], offs)
+        w_in_sb = held.tile([D, D], BF16, name="w_in_sb")
+        nc.sync.dma_start(w_in_sb[:], w_in)
         table_sb = held.tile([D, S], BF16, name="table_sb")
         nc.sync.dma_start(table_sb[:], table)
-        w_in_sb = held.tile([D, D], BF16, name="w_in_sb")
-        nc.scalar.dma_start(w_in_sb[:], w_in)
         b_in_sb = held.tile([D, 1], F32, name="b_in_sb")
-        nc.scalar.dma_start(b_in_sb[:], b_in)
+        nc.sync.dma_start(b_in_sb[:], b_in)
         dyn_sb = held.tile([D, R], F32, name="dyn_sb")
-        nc.scalar.dma_start(dyn_sb[:], dyn)
+        nc.sync.dma_start(dyn_sb[:], dyn)
         h_sb = held.tile([D, R], BF16, name="h_sb")
-        nc.scalar.dma_start(h_sb[:], h)
+        nc.sync.dma_start(h_sb[:], h)
         wf_sb = held.tile([D, 2, D], BF16, name="wf_sb")
-        nc.scalar.dma_start(wf_sb[:], wf.rearrange("(b k) m -> k b m", b=2))
+        nc.sync.dma_start(wf_sb[:], wf.rearrange("(b k) m -> k b m", b=2))
         b_f_sb = held.tile([D, 1], F32, name="b_f_sb")
         nc.sync.dma_start(b_f_sb[:], b_f)
         wh_sb = held.tile([D, 2, D], BF16, name="wh_sb")

@@ -21,6 +21,10 @@ def tile_tspddecoder_kernel(tc, table, w_in, dyn, b_in, h, wf, b_f, wh, b_h, off
         tc.tile_pool(name="held", bufs=1) as held,
         tc.psum_pool(name="psum", bufs=1) as psum,
     ):
+        warm_up = held.tile([D, 1], F32, name="warm_up")
+        nc.vector.memset(warm_up[:], 0.0)
+        nc.scalar.activation(warm_up[:], warm_up[:], FUNC.Sigmoid)
+
         offsets = held.tile([D, N // PER_COLUMN], U16, name="offsets")
         nc.sync.dma_start(offsets[:], offs)
         w_in_sb = held.tile([D, D], BF16, name="w_in_sb")

@@ -5,7 +5,7 @@ S = 1024
 R = 128
 N = 2 * R
 PER_COLUMN = 16
-GROUPS = 2
+GROUPS = 4
 G = R // GROUPS
 
 BF16, F32, U16 = mybir.dt.bfloat16, mybir.dt.float32, mybir.dt.uint16
@@ -25,12 +25,12 @@ def tile_tspddecoder_kernel(tc, table, w_in, dyn, b_in, h, wf, b_f, wh, b_h, off
         nc.vector.memset(warm_up[:], 0.0)
         nc.scalar.activation(warm_up[:], warm_up[:], FUNC.Sigmoid)
 
+        table_sb = held.tile([D, S], BF16, name="table_sb")
+        nc.sync.dma_start(table_sb[:], table)
         offsets = held.tile([D, N // PER_COLUMN], U16, name="offsets")
         nc.sync.dma_start(offsets[:], offs)
         w_in_sb = held.tile([D, D], BF16, name="w_in_sb")
         nc.sync.dma_start(w_in_sb[:], w_in)
-        table_sb = held.tile([D, S], BF16, name="table_sb")
-        nc.sync.dma_start(table_sb[:], table)
         b_in_sb = held.tile([D, 1], F32, name="b_in_sb")
         nc.sync.dma_start(b_in_sb[:], b_in)
         dyn_sb = held.tile([D, R], F32, name="dyn_sb")
@@ -55,7 +55,7 @@ def tile_tspddecoder_kernel(tc, table, w_in, dyn, b_in, h, wf, b_f, wh, b_h, off
 
         groups = [slice(g * G, (g + 1) * G) for g in range(GROUPS)]
         f_sum = [psum.tile([D, G], F32, name=f"f_sum{g}") for g in range(GROUPS)]
-        t_sum = [psum.tile([D, G], F32, name=f"t_sum{g}") for g in range(GROUPS)]
+        t_sum = [psum.tile([D, G], F32, name=f"t_sum{g}", tag="proj" if g == GROUPS - 1 else f"t_sum{g}") for g in range(GROUPS)]
         x = held.tile([D, R], BF16, name="x")
         f = held.tile([D, R], F32, name="f")
         fh = held.tile([D, R], BF16, name="fh")

@@ -25,6 +25,8 @@ def tile_tspddecoder_kernel(tc, table, w_in, dyn, b_in, h, wf, b_f, wh, b_h, off
         nc.vector.memset(warm_up[:], 0.0)
         nc.scalar.activation(warm_up[:], warm_up[:], FUNC.Sigmoid)
 
+        b_f_sb = held.tile([D, 1], F32, name="b_f_sb")
+        nc.gpsimd.dma_start(b_f_sb[:], b_f)
         table_sb = held.tile([D, S], BF16, name="table_sb")
         nc.sync.dma_start(table_sb[:], table)
         offsets = held.tile([D, N // PER_COLUMN], U16, name="offsets")
@@ -39,8 +41,6 @@ def tile_tspddecoder_kernel(tc, table, w_in, dyn, b_in, h, wf, b_f, wh, b_h, off
         nc.sync.dma_start(h_sb[:], h)
         wf_sb = held.tile([D, 2, D], BF16, name="wf_sb")
         nc.sync.dma_start(wf_sb[:], wf.rearrange("(b k) m -> k b m", b=2))
-        b_f_sb = held.tile([D, 1], F32, name="b_f_sb")
-        nc.sync.dma_start(b_f_sb[:], b_f)
         wh_sb = held.tile([D, 2, D], BF16, name="wh_sb")
         nc.sync.dma_start(wh_sb[:], wh.rearrange("(b k) m -> k b m", b=2))
         b_h_sb = held.tile([D, 1], F32, name="b_h_sb")

@@ -29,10 +29,10 @@ def tile_tspddecoder_kernel(tc, table, w_in, dyn, b_in, h, wf, b_f, wh, b_h, off
         nc.gpsimd.dma_start(b_f_sb[:], b_f)
         table_sb = held.tile([D, S], BF16, name="table_sb")
         nc.sync.dma_start(table_sb[:], table)
-        offsets = held.tile([D, N // PER_COLUMN], U16, name="offsets")
-        nc.sync.dma_start(offsets[:], offs)
         w_in_sb = held.tile([D, D], BF16, name="w_in_sb")
         nc.sync.dma_start(w_in_sb[:], w_in)
+        offsets = held.tile([D, N // PER_COLUMN], U16, name="offsets")
+        nc.sync.dma_start(offsets[:], offs)
         b_in_sb = held.tile([D, 1], F32, name="b_in_sb")
         nc.sync.dma_start(b_in_sb[:], b_in)
         dyn_sb = held.tile([D, R], F32, name="dyn_sb")

@@ -7,6 +7,7 @@ N = 2 * R
 PER_COLUMN = 16
 GROUPS = 4
 G = R // GROUPS
+DMA_ALIGN = 256
 
 BF16, F32, U16 = mybir.dt.bfloat16, mybir.dt.float32, mybir.dt.uint16
 ALU = mybir.AluOpType
@@ -27,21 +28,21 @@ def tile_tspddecoder_kernel(tc, table, w_in, dyn, b_in, h, wf, b_f, wh, b_h, off
 
         b_f_sb = held.tile([D, 1], F32, name="b_f_sb")
         nc.gpsimd.dma_start(b_f_sb[:], b_f)
-        table_sb = held.tile([D, S], BF16, name="table_sb")
+        table_sb = held.tile([D, S], BF16, name="table_sb", align_bytes=DMA_ALIGN)
         nc.sync.dma_start(table_sb[:], table)
-        w_in_sb = held.tile([D, D], BF16, name="w_in_sb")
+        w_in_sb = held.tile([D, D], BF16, name="w_in_sb", align_bytes=DMA_ALIGN)
         nc.sync.dma_start(w_in_sb[:], w_in)
         offsets = held.tile([D, N // PER_COLUMN], U16, name="offsets")
         nc.sync.dma_start(offsets[:], offs)
         b_in_sb = held.tile([D, 1], F32, name="b_in_sb")
         nc.sync.dma_start(b_in_sb[:], b_in)
-        dyn_sb = held.tile([D, R], F32, name="dyn_sb")
+        dyn_sb = held.tile([D, R], F32, name="dyn_sb", align_bytes=DMA_ALIGN)
         nc.sync.dma_start(dyn_sb[:], dyn)
-        h_sb = held.tile([D, R], BF16, name="h_sb")
+        h_sb = held.tile([D, R], BF16, name="h_sb", align_bytes=DMA_ALIGN)
         nc.sync.dma_start(h_sb[:], h)
-        wf_sb = held.tile([D, 2, D], BF16, name="wf_sb")
+        wf_sb = held.tile([D, 2, D], BF16, name="wf_sb", align_bytes=DMA_ALIGN)
         nc.sync.dma_start(wf_sb[:], wf.rearrange("(b k) m -> k b m", b=2))
-        wh_sb = held.tile([D, 2, D], BF16, name="wh_sb")
+        wh_sb = held.tile([D, 2, D], BF16, name="wh_sb", align_bytes=DMA_ALIGN)
         nc.sync.dma_start(wh_sb[:], wh.rearrange("(b k) m -> k b m", b=2))
         b_h_sb = held.tile([D, 1], F32, name="b_h_sb")
         nc.sync.dma_start(b_h_sb[:], b_h)
@@ -62,7 +63,7 @@ def tile_tspddecoder_kernel(tc, table, w_in, dyn, b_in, h, wf, b_f, wh, b_h, off
         t = held.tile([D, R], F32, name="t")
         minus_kept = held.tile([D, R], F32, name="minus_kept")
         ft = held.tile([D, R], F32, name="ft")
-        new_h = held.tile([D, R], F32, name="new_h")
+        new_h = held.tile([D, R], F32, name="new_h", align_bytes=DMA_ALIGN)
 
         for cols in groups:
             nc.vector.scalar_tensor_tensor(x[:, cols], proj[:, cols], 0.5, context[:, cols], ALU.mult, ALU.add)

@@ -34,10 +34,10 @@ def tile_tspddecoder_kernel(tc, table, w_in, dyn, b_in, h, wf, b_f, wh, b_h, off
         nc.sync.dma_start(w_in_sb[:], w_in)
         offsets = held.tile([D, N // PER_COLUMN], U16, name="offsets")
         nc.sync.dma_start(offsets[:], offs)
-        b_in_sb = held.tile([D, 1], F32, name="b_in_sb")
-        nc.sync.dma_start(b_in_sb[:], b_in)
         dyn_sb = held.tile([D, R], F32, name="dyn_sb", align_bytes=DMA_ALIGN)
         nc.sync.dma_start(dyn_sb[:], dyn)
+        b_in_sb = held.tile([D, 1], F32, name="b_in_sb")
+        nc.sync.dma_start(b_in_sb[:], b_in)
         h_sb = held.tile([D, R], BF16, name="h_sb", align_bytes=DMA_ALIGN)
         nc.sync.dma_start(h_sb[:], h)
         wf_sb = held.tile([D, 2, D], BF16, name="wf_sb", align_bytes=DMA_ALIGN)

import concourse.mybir as mybir

D = 128
S = 1024
R = 128
N = 2 * R
PER_COLUMN = 16
GROUPS = 4
G = R // GROUPS
DMA_ALIGN = 256

BF16, F32, U16 = mybir.dt.bfloat16, mybir.dt.float32, mybir.dt.uint16
ALU = mybir.AluOpType
FUNC = mybir.ActivationFunctionType

FLOPS = 2 * D * D * N + 2 * (2 * (2 * D) * D * R)


def tile_tspddecoder_kernel(tc, table, w_in, dyn, b_in, h, wf, b_f, wh, b_h, offs, out):
    nc = tc.nc
    with (
        tc.tile_pool(name="held", bufs=1) as held,
        tc.psum_pool(name="psum", bufs=1) as psum,
    ):
        warm_up = held.tile([D, 1], F32, name="warm_up")
        nc.vector.memset(warm_up[:], 0.0)
        nc.scalar.activation(warm_up[:], warm_up[:], FUNC.Sigmoid)

        b_f_sb = held.tile([D, 1], F32, name="b_f_sb")
        nc.gpsimd.dma_start(b_f_sb[:], b_f)
        table_sb = held.tile([D, S], BF16, name="table_sb", align_bytes=DMA_ALIGN)
        nc.sync.dma_start(table_sb[:], table)
        w_in_sb = held.tile([D, D], BF16, name="w_in_sb", align_bytes=DMA_ALIGN)
        nc.sync.dma_start(w_in_sb[:], w_in)
        offsets = held.tile([D, N // PER_COLUMN], U16, name="offsets")
        nc.sync.dma_start(offsets[:], offs)
        dyn_sb = held.tile([D, R], F32, name="dyn_sb", align_bytes=DMA_ALIGN)
        nc.sync.dma_start(dyn_sb[:], dyn)
        b_in_sb = held.tile([D, 1], F32, name="b_in_sb")
        nc.sync.dma_start(b_in_sb[:], b_in)
        h_sb = held.tile([D, R], BF16, name="h_sb", align_bytes=DMA_ALIGN)
        nc.sync.dma_start(h_sb[:], h)
        wf_sb = held.tile([D, 2, D], BF16, name="wf_sb", align_bytes=DMA_ALIGN)
        nc.sync.dma_start(wf_sb[:], wf.rearrange("(b k) m -> k b m", b=2))
        wh_sb = held.tile([D, 2, D], BF16, name="wh_sb", align_bytes=DMA_ALIGN)
        nc.sync.dma_start(wh_sb[:], wh.rearrange("(b k) m -> k b m", b=2))
        b_h_sb = held.tile([D, 1], F32, name="b_h_sb")
        nc.sync.dma_start(b_h_sb[:], b_h)

        half = R // PER_COLUMN
        proj = psum.tile([D, R], F32, name="proj")
        nc.tensor.matmul(proj[:], w_in_sb[:], table_sb[:].indirect(offsets[:, 0:half]), start=True, stop=False)
        nc.tensor.matmul(proj[:], w_in_sb[:], table_sb[:].indirect(offsets[:, half : 2 * half]), start=False, stop=True)
        context = held.tile([D, R], F32, name="context")
        nc.vector.tensor_scalar_add(context[:], dyn_sb[:], b_in_sb[:, 0:1])

        groups = [slice(g * G, (g + 1) * G) for g in range(GROUPS)]
        f_sum = [psum.tile([D, G], F32, name=f"f_sum{g}") for g in range(GROUPS)]
        t_sum = [psum.tile([D, G], F32, name=f"t_sum{g}", tag="proj" if g == GROUPS - 1 else f"t_sum{g}") for g in range(GROUPS)]
        x = held.tile([D, R], BF16, name="x")
        f = held.tile([D, R], F32, name="f")
        fh = held.tile([D, R], BF16, name="fh")
        t = held.tile([D, R], F32, name="t")
        minus_kept = held.tile([D, R], F32, name="minus_kept")
        ft = held.tile([D, R], F32, name="ft")
        new_h = held.tile([D, R], F32, name="new_h", align_bytes=DMA_ALIGN)

        for cols in groups:
            nc.vector.scalar_tensor_tensor(x[:, cols], proj[:, cols], 0.5, context[:, cols], ALU.mult, ALU.add)

        for g, cols in enumerate(groups):
            nc.tensor.matmul(f_sum[g][:], wf_sb[:, 0, :], h_sb[:, cols], start=True, stop=False)
        for g, cols in enumerate(groups):
            nc.tensor.matmul(f_sum[g][:], wf_sb[:, 1, :], x[:, cols], start=False, stop=True)
        for g, cols in enumerate(groups):
            nc.scalar.activation(f[:, cols], f_sum[g][:], FUNC.Sigmoid, bias=b_f_sb[:, 0:1])

        for cols in groups:
            nc.vector.tensor_mul(fh[:, cols], f[:, cols], h_sb[:, cols])
        for g, cols in enumerate(groups):
            nc.tensor.matmul(t_sum[g][:], wh_sb[:, 1, :], x[:, cols], start=True, stop=False)
        for g, cols in enumerate(groups):
            nc.tensor.matmul(t_sum[g][:], wh_sb[:, 0, :], fh[:, cols], start=False, stop=True)
        for g, cols in enumerate(groups):
            nc.scalar.activation(t[:, cols], t_sum[g][:], FUNC.Tanh, bias=b_h_sb[:, 0:1])

        nc.vector.scalar_tensor_tensor(minus_kept[:], f[:], 1.0, h_sb[:], ALU.subtract, ALU.mult)
        for cols in groups:
            nc.vector.tensor_mul(ft[:, cols], f[:, cols], t[:, cols])
        for cols in groups:
            nc.vector.tensor_sub(new_h[:, cols], ft[:, cols], minus_kept[:, cols])
        nc.sync.dma_start(out, new_h[:])
